import numpy as np
import ml_dtypes


def mxq(x, axis, fmt="e4m3"):
    dtype, down = {"e4m3": (ml_dtypes.float8_e4m3fn, 7), "e5m2": (ml_dtypes.float8_e5m2, 14)}[fmt]
    v = np.moveaxis(np.asarray(x, np.float32).astype(ml_dtypes.bfloat16).astype(np.float64), axis, -1)
    blocks = v.reshape(v.shape[:-1] + (-1, 32))
    amax = np.abs(blocks).max(-1, keepdims=True)
    byte = np.maximum(np.where(amax > 0, np.frexp(amax)[1] - 1 + 127, 0) - down, 1)
    scale = np.exp2(byte - 127.0)
    codes = (blocks / scale).astype(np.float32).astype(dtype).astype(np.float64)
    return np.moveaxis((codes * scale).reshape(v.shape), -1, axis)


WIDE = False


def mx_kscale(k):
    if not WIDE:
        return np.ones(k)
    levels = np.array([10, -10, 5, -5, 0])
    a = np.random.permutation(np.resize(levels, k // 512 * 4)).reshape(k // 512, 4)
    idx = np.arange(k)
    return np.exp2(a[idx // 512, idx % 128 // 32])


BF16 = ml_dtypes.bfloat16


def bf(x):
    return np.asarray(x, np.float32).astype(BF16)


def f64(x):
    return np.asarray(x).astype(np.float64)


E2M1 = np.array([0.0, 0.5, 1.0, 1.5, 2.0, 3.0, 4.0, 6.0, -0.0, -0.5, -1.0, -1.5, -2.0, -3.0, -4.0, -6.0])


def pack_weight(w, fmt):
    k, n = w.shape
    w = f64(bf(w)).reshape(k // 32, 32, n)
    amax = np.abs(w).max(1)
    if fmt == "e4m3":
        byte = np.frexp(amax)[1] - 1 + 127 - 7
    else:
        mant, ex = np.frexp(amax / 6.0)
        byte = np.where(mant > 0.5, ex, ex - 1) + 127
    byte = np.clip(np.where(amax > 0, byte, 1), 1, 254)
    scaled = (w * np.exp2(127.0 - byte)[:, None, :]).reshape(k, n).astype(np.float32)
    by_word = np.ascontiguousarray(scaled.reshape(k // 512, 128, 4, n).transpose(0, 1, 3, 2))
    if fmt == "e4m3":
        words = by_word.astype(ml_dtypes.float8_e4m3fn).view(np.uint8)
    else:
        c = by_word.astype(ml_dtypes.float4_e2m1fn).view(np.uint8) & 0xF
        words = c[..., 0::2] | (c[..., 1::2] << 4)
    return np.ascontiguousarray(words), np.ascontiguousarray(byte.astype(np.uint8).reshape(k // 512, 16, n))


def unpack_weight(words, scales, fmt):
    g, p, n, _ = words.shape
    if fmt == "e4m3":
        vals = np.ascontiguousarray(words).view(ml_dtypes.float8_e4m3fn).astype(np.float64)
    else:
        nib = np.empty((g, p, n, 4), np.uint8)
        nib[..., 0::2] = words & 0xF
        nib[..., 1::2] = words >> 4
        vals = E2M1[nib]
    vals = vals * np.repeat(np.exp2(scales.astype(np.float64) - 127.0), 8, axis=1)[..., None]
    return vals.transpose(0, 1, 3, 2).reshape(g * 512, n)

def pack4(w):
    words, scales = pack_weight(w, "e2m1")
    return words.reshape(words.shape[0], 128, -1), scales


def unpack4(words, scales):
    return unpack_weight(words.reshape(words.shape[0], 128, -1, 2), scales, "e2m1")


B, C, H, D, N, CO = 16, 128, 2048, 512, 4, 128
NC = N * C
EPS = 1e-5


def bn(v, gamma, beta, axes):
    mean = v.mean(axis=axes, keepdims=True)
    var = v.var(axis=axes, keepdims=True)
    return (v - mean) / np.sqrt(var + EPS) * gamma + beta


def setup_inputs():
    u = mx_kscale(NC)
    head = np.maximum(np.random.standard_normal((N, B, C, D)), 0.0) + 0.25 * np.random.standard_normal((N, B, C, D))
    w = np.random.standard_normal((CO, NC)) / np.sqrt(NC) / u[None, :]
    words, scales = pack4(np.ascontiguousarray(w.T))
    return {'head_res': bf(head * u.reshape(N, 1, C, 1)),
            'W_merge_words': words,
            'W_merge_scales': scales,
            'g_m': bf(1.0 + 0.1 * np.random.standard_normal(CO)),
            'b_m': bf(0.1 * np.random.standard_normal(CO))}


def reference(head_res, W_merge_words, W_merge_scales, g_m, b_m):
    cat = f64(head_res).transpose(1, 0, 2, 3).reshape(B, NC, D)
    m = unpack4(W_merge_words, W_merge_scales).T[None] @ mxq(cat, 1, 'e4m3')
    m = bn(m, f64(g_m)[None, :, None], f64(b_m)[None, :, None], (0, 2))
    return np.maximum(m, 0.0)

@@ -1,0 +1,179 @@
+from contextlib import ExitStack
+
+import concourse.mybir as mybir
+
+BF16 = mybir.dt.bfloat16
+F32 = mybir.dt.float32
+I32 = mybir.dt.int32
+U8 = mybir.dt.uint8
+U32 = mybir.dt.uint32
+FP8X4 = mybir.dt.float8_e4m3fn_x4
+FP4X4 = mybir.dt.float4_e2m1fn_x4
+ALU = mybir.AluOpType
+ACT = mybir.ActivationFunctionType
+
+HEADS = 4
+SAMPLES = 16
+CHANNELS = 128
+POSITIONS = 512
+OUT_CHANNELS = 128
+EPS = 1e-5
+
+P = 128
+PACK = 4
+QUADRANT = CHANNELS // PACK
+LANES = P // QUADRANT
+GROUPS = SAMPLES // LANES
+SLABS = GROUPS * HEADS
+BANKS = 8
+
+SCALAR_COLUMNS = 336
+RUN = 4
+STATS_LAG = LANES + 1
+
+FLOPS = 2 * SAMPLES * OUT_CHANNELS * HEADS * CHANNELS * POSITIONS
+
+
+def tile_block_height_reducing_filtering_pb_t_kernel(
+    tc, head_res, W_merge_words, W_merge_scales, g_m, b_m, out
+):
+    nc = tc.nc
+    with ExitStack() as ctx:
+        consts = ctx.enter_context(tc.tile_pool(name="consts", bufs=1))
+        raw_pool = ctx.enter_context(tc.tile_pool(name="raw", bufs=SLABS))
+        grouped_pool = ctx.enter_context(tc.tile_pool(name="grouped", bufs=4))
+        result_pool = ctx.enter_context(tc.tile_pool(name="result", bufs=SAMPLES))
+        psum = ctx.enter_context(tc.psum_pool(name="sums", bufs=BANKS))
+        ctx.enter_context(tc.manual_schedule())
+
+        w_words = consts.tile([P, HEADS, LANES, 2 * OUT_CHANNELS], U8, align_bytes=64)
+        w_scales = consts.tile([P, HEADS, LANES, OUT_CHANNELS], U8, align_bytes=64)
+        nc.vector.memset(w_words[:].rearrange("p n j w -> p (n j w)").bitcast(I32), 0)
+        nc.vector.memset(w_scales[:].rearrange("p n j o -> p (n j o)").bitcast(I32), 0)
+        eps = consts.tile([P, 1], F32)
+        nc.vector.memset(eps[:], EPS)
+        warm = consts.tile([P, 1], F32)
+        nc.scalar.activation(out=warm[:], in_=eps[:], func=ACT.Sqrt)
+
+        slabs = head_res.rearrange("n (g j) (q t) d -> g n (j q) (t d)", j=LANES, t=PACK)
+        raw = {}
+
+        def load(r):
+            raw[r] = raw_pool.tile([P, PACK, POSITIONS], BF16, name="raw")
+            nc.sync.dma_start(
+                out=raw[r][:].rearrange("p t d -> p (t d)"), in_=slabs[r // HEADS, r % HEADS]
+            )
+
+        words_by_head = W_merge_words[0].rearrange("(n q) w -> q n w", n=HEADS)
+        scales_by_head = W_merge_scales[0].rearrange("(n i) o -> i n o", n=HEADS)
+        FIRST_LOADS = 3
+        for r in range(FIRST_LOADS):
+            load(r)
+        for j in range(LANES):
+            nc.sync.dma_start(
+                out=w_words[QUADRANT * j : QUADRANT * (j + 1), :, j, :].bitcast(I32),
+                in_=words_by_head.bitcast(I32),
+            )
+        for j in range(LANES):
+            nc.sync.dma_start(
+                out=w_scales[QUADRANT * j : QUADRANT * j + 4, :, j, :].bitcast(I32),
+                in_=scales_by_head.bitcast(I32),
+            )
+        for r in range(FIRST_LOADS, SLABS):
+            load(r)
+        g_bf = consts.tile([P, 1], BF16)
+        b_bf = consts.tile([P, 1], BF16)
+        with nc.allow_non_contiguous_dma(reason="128 two-byte elements, one to a partition"):
+            nc.sync.dma_start(out=g_bf[:], in_=g_m.rearrange("(o one) -> o one", one=1))
+            nc.sync.dma_start(out=b_bf[:], in_=b_m.rearrange("(o one) -> o one", one=1))
+
+        codes = consts.tile([P, SLABS, POSITIONS], U32, align_bytes=64)
+        planes = consts.tile([P, SLABS, POSITIONS], U8, align_bytes=64)
+        stats = consts.tile([P, SAMPLES, 6], F32)
+        grouped = {}
+        banks = {}
+
+        def regroup(r):
+            grouped[r] = grouped_pool.tile([P, POSITIONS, PACK], BF16, name="grouped", align_bytes=64)
+            src = raw[r][:].rearrange("p t (c i) -> p c t i", i=RUN)
+            dst = grouped[r][:].rearrange("p (c i) t -> p c t i", i=RUN)
+            cut = SCALAR_COLUMNS // RUN
+            nc.scalar.copy(out=dst[:, :cut], in_=src[:, :cut])
+            nc.vector.tensor_copy(out=dst[:, cut:], in_=src[:, cut:])
+
+        def quantise(r):
+            nc.vector.quantize_mx(
+                out=codes[:, r, :].bitcast(FP8X4),
+                scales=planes[:, r, :],
+                in_=grouped[r][:].rearrange("p d t -> p (d t)"),
+            )
+
+        def multiply(bank, g, n, j):
+            r = g * HEADS + n
+            nc.tensor.matmul_mx(
+                out=bank[:],
+                lhsT=w_words[:, n, j, :].bitcast(FP4X4),
+                lhsT_scale=w_scales[:, n, j, :],
+                rhs=codes[:, r, :].bitcast(FP8X4),
+                rhs_scale=planes[:, r, :],
+                start=(n == 0),
+                stop=(n == HEADS - 1),
+            )
+
+        def multiply_slab(r):
+            g, n = r // HEADS, r % HEADS
+            for j in range(LANES):
+                if n == 0:
+                    banks[g * LANES + j] = psum.tile([P, POSITIONS], F32, name="bank")
+                multiply(banks[g * LANES + j], g, n, j)
+
+        def statistics(sample):
+            nc.vector.bn_stats(out=stats[:, sample, :], in_=banks[sample][:])
+
+        for r in range(SLABS):
+            regroup(r)
+            if r >= 1:
+                quantise(r - 1)
+                multiply_slab(r - 1)
+            if r >= STATS_LAG:
+                statistics(r - STATS_LAG)
+        quantise(SLABS - 1)
+        multiply_slab(SLABS - 1)
+        for sample in range(SLABS - STATS_LAG, SAMPLES):
+            statistics(sample)
+
+        mean_var = consts.tile([P, 2], F32)
+        nc.vector.bn_aggr(out=mean_var[:], in_=stats[:].rearrange("p s c -> p (s c)"))
+        std = consts.tile([P, 1], F32)
+        nc.scalar.activation(out=std[:], in_=mean_var[:, 1:2], func=ACT.Sqrt, bias=eps[:], scale=1.0)
+        minus_g_mean = consts.tile([P, 1], F32)
+        nc.vector.tensor_scalar(
+            out=minus_g_mean[:], in0=mean_var[:, 0:1], scalar1=g_bf[:], scalar2=-1.0, op0=ALU.mult, op1=ALU.mult
+        )
+        rstd = consts.tile([P, 1], F32)
+        nc.vector.reciprocal(out=rstd[:], in_=std[:])
+        gain = consts.tile([P, 1], F32)
+        nc.vector.tensor_mul(out=gain[:], in0=g_bf[:], in1=rstd[:])
+        shift = consts.tile([P, 1], F32)
+        nc.vector.scalar_tensor_tensor(
+            out=shift[:], in0=minus_g_mean[:], scalar=rstd[:], in1=b_bf[:], op0=ALU.mult, op1=ALU.add
+        )
+
+        def normalise(sample):
+            y = result_pool.tile([P, POSITIONS], F32, name="y")
+            if sample % 2 == 0:
+                nc.scalar.activation(out=y[:], in_=banks[sample][:], func=ACT.Relu, bias=shift[:], scale=gain[:])
+            else:
+                nc.vector.tensor_scalar(
+                    out=y[:], in0=banks[sample][:], scalar1=gain[:], scalar2=shift[:], op0=ALU.mult, op1=ALU.add
+                )
+                nc.vector.tensor_scalar_max(out=y[:], in0=y[:], scalar1=0.0)
+            nc.sync.dma_start(out=out[sample], in_=y[:])
+
+        for sample in range(SAMPLES - BANKS, SAMPLES):
+            normalise(sample)
+        for sample in range(SAMPLES - BANKS):
+            banks[sample] = psum.tile([P, POSITIONS], F32, name="bank")
+            for n in range(HEADS):
+                multiply(banks[sample], sample // LANES, n, sample % LANES)
+            normalise(sample)

@@ -23,13 +23,15 @@ P = 128
 PACK = 4
 QUADRANT = CHANNELS // PACK
 LANES = P // QUADRANT
+SCALE_ROWS = QUADRANT // 8
 GROUPS = SAMPLES // LANES
 SLABS = GROUPS * HEADS
 BANKS = 8
 
-SCALAR_COLUMNS = 336
 RUN = 4
 STATS_LAG = LANES + 1
+SCALAR_COLUMNS_BEFORE_STATS = 272
+SCALAR_COLUMNS = 368
 
 FLOPS = 2 * SAMPLES * OUT_CHANNELS * HEADS * CHANNELS * POSITIONS
 
@@ -41,15 +43,16 @@ def tile_block_height_reducing_filtering_pb_t_kernel(
     with ExitStack() as ctx:
         consts = ctx.enter_context(tc.tile_pool(name="consts", bufs=1))
         raw_pool = ctx.enter_context(tc.tile_pool(name="raw", bufs=SLABS))
-        grouped_pool = ctx.enter_context(tc.tile_pool(name="grouped", bufs=4))
+        grouped_pool = ctx.enter_context(tc.tile_pool(name="grouped", bufs=6))
+        kept_pool = ctx.enter_context(tc.tile_pool(name="kept", bufs=LANES))
         result_pool = ctx.enter_context(tc.tile_pool(name="result", bufs=SAMPLES))
         psum = ctx.enter_context(tc.psum_pool(name="sums", bufs=BANKS))
         ctx.enter_context(tc.manual_schedule())
 
+        w_scales = consts.tile([P, HEADS, OUT_CHANNELS], U8, align_bytes=64)
         w_words = consts.tile([P, HEADS, LANES, 2 * OUT_CHANNELS], U8, align_bytes=64)
-        w_scales = consts.tile([P, HEADS, LANES, OUT_CHANNELS], U8, align_bytes=64)
+        nc.vector.memset(w_scales[:].rearrange("p n o -> p (n o)").bitcast(I32), 0)
         nc.vector.memset(w_words[:].rearrange("p n j w -> p (n j w)").bitcast(I32), 0)
-        nc.vector.memset(w_scales[:].rearrange("p n j o -> p (n j o)").bitcast(I32), 0)
         eps = consts.tile([P, 1], F32)
         nc.vector.memset(eps[:], EPS)
         warm = consts.tile([P, 1], F32)
@@ -66,20 +69,20 @@ def tile_block_height_reducing_filtering_pb_t_kernel(
 
         words_by_head = W_merge_words[0].rearrange("(n q) w -> q n w", n=HEADS)
         scales_by_head = W_merge_scales[0].rearrange("(n i) o -> i n o", n=HEADS)
-        FIRST_LOADS = 3
-        for r in range(FIRST_LOADS):
+        load(0)
+        for j in range(LANES):
+            nc.sync.dma_start(
+                out=w_scales[QUADRANT * j : QUADRANT * j + SCALE_ROWS, :, :].bitcast(I32),
+                in_=scales_by_head.bitcast(I32),
+            )
+        for r in range(1, LANES):
             load(r)
         for j in range(LANES):
             nc.sync.dma_start(
                 out=w_words[QUADRANT * j : QUADRANT * (j + 1), :, j, :].bitcast(I32),
                 in_=words_by_head.bitcast(I32),
             )
-        for j in range(LANES):
-            nc.sync.dma_start(
-                out=w_scales[QUADRANT * j : QUADRANT * j + 4, :, j, :].bitcast(I32),
-                in_=scales_by_head.bitcast(I32),
-            )
-        for r in range(FIRST_LOADS, SLABS):
+        for r in range(LANES, SLABS):
             load(r)
         g_bf = consts.tile([P, 1], BF16)
         b_bf = consts.tile([P, 1], BF16)
@@ -92,12 +95,13 @@ def tile_block_height_reducing_filtering_pb_t_kernel(
         stats = consts.tile([P, SAMPLES, 6], F32)
         grouped = {}
         banks = {}
+        kept = {}
 
         def regroup(r):
             grouped[r] = grouped_pool.tile([P, POSITIONS, PACK], BF16, name="grouped", align_bytes=64)
             src = raw[r][:].rearrange("p t (c i) -> p c t i", i=RUN)
             dst = grouped[r][:].rearrange("p (c i) t -> p c t i", i=RUN)
-            cut = SCALAR_COLUMNS // RUN
+            cut = (SCALAR_COLUMNS_BEFORE_STATS if r < STATS_LAG else SCALAR_COLUMNS) // RUN
             nc.scalar.copy(out=dst[:, :cut], in_=src[:, :cut])
             nc.vector.tensor_copy(out=dst[:, cut:], in_=src[:, cut:])
 
@@ -108,12 +112,12 @@ def tile_block_height_reducing_filtering_pb_t_kernel(
                 in_=grouped[r][:].rearrange("p d t -> p (d t)"),
             )
 
-        def multiply(bank, g, n, j):
-            r = g * HEADS + n
+        def multiply(sample, n):
+            r = (sample // LANES) * HEADS + n
             nc.tensor.matmul_mx(
-                out=bank[:],
-                lhsT=w_words[:, n, j, :].bitcast(FP4X4),
-                lhsT_scale=w_scales[:, n, j, :],
+                out=banks[sample][:],
+                lhsT=w_words[:, n, sample % LANES, :].bitcast(FP4X4),
+                lhsT_scale=w_scales[:, n, :],
                 rhs=codes[:, r, :].bitcast(FP8X4),
                 rhs_scale=planes[:, r, :],
                 start=(n == 0),
@@ -122,13 +126,22 @@ def tile_block_height_reducing_filtering_pb_t_kernel(
 
         def multiply_slab(r):
             g, n = r // HEADS, r % HEADS
-            for j in range(LANES):
+            for sample in range(g * LANES, (g + 1) * LANES):
                 if n == 0:
-                    banks[g * LANES + j] = psum.tile([P, POSITIONS], F32, name="bank")
-                multiply(banks[g * LANES + j], g, n, j)
+                    banks[sample] = psum.tile([P, POSITIONS], F32, name="bank")
+                multiply(sample, n)
+
+        def multiply_again(sample):
+            banks[sample] = psum.tile([P, POSITIONS], F32, name="bank")
+            for n in range(HEADS):
+                multiply(sample, n)
 
         def statistics(sample):
             nc.vector.bn_stats(out=stats[:, sample, :], in_=banks[sample][:])
+
+        def keep(sample):
+            kept[sample] = kept_pool.tile([P, POSITIONS], F32, name="kept")
+            nc.scalar.copy(out=kept[sample][:], in_=banks[sample][:])
 
         for r in range(SLABS):
             regroup(r)
@@ -139,7 +152,13 @@ def tile_block_height_reducing_filtering_pb_t_kernel(
                 statistics(r - STATS_LAG)
         quantise(SLABS - 1)
         multiply_slab(SLABS - 1)
-        for sample in range(SLABS - STATS_LAG, SAMPLES):
+        statistics(SLABS - STATS_LAG)
+
+        for sample in range(2 * LANES, 3 * LANES):
+            keep(sample)
+        for sample in range(LANES):
+            multiply_again(sample)
+        for sample in range(3 * LANES, SAMPLES):
             statistics(sample)
 
         mean_var = consts.tile([P, 2], F32)
@@ -159,21 +178,24 @@ def tile_block_height_reducing_filtering_pb_t_kernel(
             out=shift[:], in0=minus_g_mean[:], scalar=rstd[:], in1=b_bf[:], op0=ALU.mult, op1=ALU.add
         )
 
-        def normalise(sample):
+        def normalise_bank(sample):
             y = result_pool.tile([P, POSITIONS], F32, name="y")
-            if sample % 2 == 0:
-                nc.scalar.activation(out=y[:], in_=banks[sample][:], func=ACT.Relu, bias=shift[:], scale=gain[:])
-            else:
-                nc.vector.tensor_scalar(
-                    out=y[:], in0=banks[sample][:], scalar1=gain[:], scalar2=shift[:], op0=ALU.mult, op1=ALU.add
-                )
-                nc.vector.tensor_scalar_max(out=y[:], in0=y[:], scalar1=0.0)
+            nc.scalar.activation(out=y[:], in_=banks[sample][:], func=ACT.Relu, bias=shift[:], scale=gain[:])
             nc.sync.dma_start(out=out[sample], in_=y[:])
 
-        for sample in range(SAMPLES - BANKS, SAMPLES):
-            normalise(sample)
-        for sample in range(SAMPLES - BANKS):
-            banks[sample] = psum.tile([P, POSITIONS], F32, name="bank")
-            for n in range(HEADS):
-                multiply(banks[sample], sample // LANES, n, sample % LANES)
-            normalise(sample)
+        def normalise_kept(sample):
+            y = result_pool.tile([P, POSITIONS], F32, name="y")
+            nc.vector.tensor_scalar(
+                out=y[:], in0=kept[sample][:], scalar1=gain[:], scalar2=shift[:], op0=ALU.mult, op1=ALU.add
+            )
+            nc.vector.tensor_scalar_max(out=y[:], in0=y[:], scalar1=0.0)
+            nc.sync.dma_start(out=out[sample], in_=y[:])
+
+        for j in range(LANES):
+            normalise_bank(3 * LANES + j)
+            normalise_kept(2 * LANES + j)
+        for sample in range(LANES):
+            normalise_bank(sample)
+        for sample in range(LANES, 2 * LANES):
+            multiply_again(sample)
+            normalise_bank(sample)

@@ -31,7 +31,8 @@ BANKS = 8
 RUN = 4
 STATS_LAG = LANES + 1
 SCALAR_COLUMNS_BEFORE_STATS = 272
-SCALAR_COLUMNS = 368
+SCALAR_COLUMNS = 344
+GPSIMD_COLUMNS = 64
 
 FLOPS = 2 * SAMPLES * OUT_CHANNELS * HEADS * CHANNELS * POSITIONS
 
@@ -102,8 +103,13 @@ def tile_block_height_reducing_filtering_pb_t_kernel(
             src = raw[r][:].rearrange("p t (c i) -> p c t i", i=RUN)
             dst = grouped[r][:].rearrange("p (c i) t -> p c t i", i=RUN)
             cut = (SCALAR_COLUMNS_BEFORE_STATS if r < STATS_LAG else SCALAR_COLUMNS) // RUN
+            end = (POSITIONS if r < STATS_LAG else POSITIONS - GPSIMD_COLUMNS) // RUN
             nc.scalar.copy(out=dst[:, :cut], in_=src[:, :cut])
-            nc.vector.tensor_copy(out=dst[:, cut:], in_=src[:, cut:])
+            nc.vector.tensor_copy(out=dst[:, cut:end], in_=src[:, cut:end])
+            if r >= STATS_LAG:
+                nc.gpsimd.tensor_scalar(
+                    out=dst[:, end:], in0=src[:, end:], scalar1=1.0, scalar2=0.0, op0=ALU.mult, op1=ALU.add
+                )
 
         def quantise(r):
             nc.vector.quantize_mx(

@@ -27,12 +27,13 @@ SCALE_ROWS = QUADRANT // 8
 GROUPS = SAMPLES // LANES
 SLABS = GROUPS * HEADS
 BANKS = 8
+BN_STATS_DIM = 6
+GROUPED_BUFS = 6
 
 RUN = 4
-STATS_LAG = LANES + 1
+STATS_LAG = LANES + 2
 SCALAR_COLUMNS_BEFORE_STATS = 272
-SCALAR_COLUMNS = 344
-GPSIMD_COLUMNS = 64
+SCALAR_COLUMNS = 368
 
 FLOPS = 2 * SAMPLES * OUT_CHANNELS * HEADS * CHANNELS * POSITIONS
 
@@ -44,7 +45,7 @@ def tile_block_height_reducing_filtering_pb_t_kernel(
     with ExitStack() as ctx:
         consts = ctx.enter_context(tc.tile_pool(name="consts", bufs=1))
         raw_pool = ctx.enter_context(tc.tile_pool(name="raw", bufs=SLABS))
-        grouped_pool = ctx.enter_context(tc.tile_pool(name="grouped", bufs=6))
+        grouped_pool = ctx.enter_context(tc.tile_pool(name="grouped", bufs=GROUPED_BUFS))
         kept_pool = ctx.enter_context(tc.tile_pool(name="kept", bufs=LANES))
         result_pool = ctx.enter_context(tc.tile_pool(name="result", bufs=SAMPLES))
         psum = ctx.enter_context(tc.psum_pool(name="sums", bufs=BANKS))
@@ -93,7 +94,7 @@ def tile_block_height_reducing_filtering_pb_t_kernel(
 
         codes = consts.tile([P, SLABS, POSITIONS], U32, align_bytes=64)
         planes = consts.tile([P, SLABS, POSITIONS], U8, align_bytes=64)
-        stats = consts.tile([P, SAMPLES, 6], F32)
+        stats = consts.tile([P, SAMPLES, BN_STATS_DIM], F32)
         grouped = {}
         banks = {}
         kept = {}
@@ -103,13 +104,8 @@ def tile_block_height_reducing_filtering_pb_t_kernel(
             src = raw[r][:].rearrange("p t (c i) -> p c t i", i=RUN)
             dst = grouped[r][:].rearrange("p (c i) t -> p c t i", i=RUN)
             cut = (SCALAR_COLUMNS_BEFORE_STATS if r < STATS_LAG else SCALAR_COLUMNS) // RUN
-            end = (POSITIONS if r < STATS_LAG else POSITIONS - GPSIMD_COLUMNS) // RUN
             nc.scalar.copy(out=dst[:, :cut], in_=src[:, :cut])
-            nc.vector.tensor_copy(out=dst[:, cut:end], in_=src[:, cut:end])
-            if r >= STATS_LAG:
-                nc.gpsimd.tensor_scalar(
-                    out=dst[:, end:], in0=src[:, end:], scalar1=1.0, scalar2=0.0, op0=ALU.mult, op1=ALU.add
-                )
+            nc.vector.tensor_copy(out=dst[:, cut:], in_=src[:, cut:])
 
         def quantise(r):
             nc.vector.quantize_mx(
@@ -158,13 +154,14 @@ def tile_block_height_reducing_filtering_pb_t_kernel(
                 statistics(r - STATS_LAG)
         quantise(SLABS - 1)
         multiply_slab(SLABS - 1)
-        statistics(SLABS - STATS_LAG)
+        for sample in range(SLABS - STATS_LAG, (GROUPS - 1) * LANES):
+            statistics(sample)
 
-        for sample in range(2 * LANES, 3 * LANES):
+        for sample in range((GROUPS - 2) * LANES, (GROUPS - 1) * LANES):
             keep(sample)
         for sample in range(LANES):
             multiply_again(sample)
-        for sample in range(3 * LANES, SAMPLES):
+        for sample in range((GROUPS - 1) * LANES, SAMPLES):
             statistics(sample)
 
         mean_var = consts.tile([P, 2], F32)
@@ -198,8 +195,8 @@ def tile_block_height_reducing_filtering_pb_t_kernel(
             nc.sync.dma_start(out=out[sample], in_=y[:])
 
         for j in range(LANES):
-            normalise_bank(3 * LANES + j)
-            normalise_kept(2 * LANES + j)
+            normalise_bank((GROUPS - 1) * LANES + j)
+            normalise_kept((GROUPS - 2) * LANES + j)
         for sample in range(LANES):
             normalise_bank(sample)
         for sample in range(LANES, 2 * LANES):

@@ -28,12 +28,15 @@ GROUPS = SAMPLES // LANES
 SLABS = GROUPS * HEADS
 BANKS = 8
 BN_STATS_DIM = 6
-GROUPED_BUFS = 6
+EVEN_BUFS = 2
+ODD_BUFS = 1
 
 RUN = 4
-STATS_LAG = LANES + 2
-SCALAR_COLUMNS_BEFORE_STATS = 272
-SCALAR_COLUMNS = 368
+FIRST_STATS_STEP = LANES + 2
+SLAB_0_SCALAR_COLUMNS = 176
+SLAB_1_SCALAR_COLUMNS = 272
+SHARED_SCALAR_COLUMNS = 160
+GPSIMD_COLUMNS = 208
 
 FLOPS = 2 * SAMPLES * OUT_CHANNELS * HEADS * CHANNELS * POSITIONS
 
@@ -45,7 +48,8 @@ def tile_block_height_reducing_filtering_pb_t_kernel(
     with ExitStack() as ctx:
         consts = ctx.enter_context(tc.tile_pool(name="consts", bufs=1))
         raw_pool = ctx.enter_context(tc.tile_pool(name="raw", bufs=SLABS))
-        grouped_pool = ctx.enter_context(tc.tile_pool(name="grouped", bufs=GROUPED_BUFS))
+        even_pool = ctx.enter_context(tc.tile_pool(name="grouped_even", bufs=EVEN_BUFS))
+        odd_pool = ctx.enter_context(tc.tile_pool(name="grouped_odd", bufs=ODD_BUFS))
         kept_pool = ctx.enter_context(tc.tile_pool(name="kept", bufs=LANES))
         result_pool = ctx.enter_context(tc.tile_pool(name="result", bufs=SAMPLES))
         psum = ctx.enter_context(tc.psum_pool(name="sums", bufs=BANKS))
@@ -99,13 +103,36 @@ def tile_block_height_reducing_filtering_pb_t_kernel(
         banks = {}
         kept = {}
 
+        def shares(r):
+            if r == 0:
+                return SLAB_0_SCALAR_COLUMNS, SLAB_0_SCALAR_COLUMNS
+            if r == 1:
+                return SLAB_1_SCALAR_COLUMNS, SLAB_1_SCALAR_COLUMNS
+            if r % 2 == 0:
+                return POSITIONS, POSITIONS
+            if r <= FIRST_STATS_STEP:
+                return 0, 0
+            return SHARED_SCALAR_COLUMNS, SHARED_SCALAR_COLUMNS + GPSIMD_COLUMNS
+
         def regroup(r):
-            grouped[r] = grouped_pool.tile([P, POSITIONS, PACK], BF16, name="grouped", align_bytes=64)
+            pool = odd_pool if r % 2 else even_pool
+            grouped[r] = pool.tile([P, POSITIONS, PACK], BF16, name="grouped", align_bytes=64)
             src = raw[r][:].rearrange("p t (c i) -> p c t i", i=RUN)
             dst = grouped[r][:].rearrange("p (c i) t -> p c t i", i=RUN)
-            cut = (SCALAR_COLUMNS_BEFORE_STATS if r < STATS_LAG else SCALAR_COLUMNS) // RUN
-            nc.scalar.copy(out=dst[:, :cut], in_=src[:, :cut])
-            nc.vector.tensor_copy(out=dst[:, cut:], in_=src[:, cut:])
+            first, second = shares(r)
+            if first > 0:
+                nc.scalar.copy(out=dst[:, : first // RUN], in_=src[:, : first // RUN])
+            if second < POSITIONS:
+                nc.vector.tensor_copy(out=dst[:, second // RUN :], in_=src[:, second // RUN :])
+            if second > first:
+                nc.gpsimd.tensor_scalar(
+                    out=grouped[r][:, first:second, :],
+                    in0=raw[r][:, :, first:second].rearrange("p t d -> p d t"),
+                    scalar1=1.0,
+                    scalar2=0.0,
+                    op0=ALU.mult,
+                    op1=ALU.add,
+                )
 
         def quantise(r):
             nc.vector.quantize_mx(
@@ -145,17 +172,16 @@ def tile_block_height_reducing_filtering_pb_t_kernel(
             kept[sample] = kept_pool.tile([P, POSITIONS], F32, name="kept")
             nc.scalar.copy(out=kept[sample][:], in_=banks[sample][:])
 
-        for r in range(SLABS):
-            regroup(r)
-            if r >= 1:
-                quantise(r - 1)
-                multiply_slab(r - 1)
-            if r >= STATS_LAG:
-                statistics(r - STATS_LAG)
-        quantise(SLABS - 1)
-        multiply_slab(SLABS - 1)
-        for sample in range(SLABS - STATS_LAG, (GROUPS - 1) * LANES):
-            statistics(sample)
+        regroup(0)
+        regroup(1)
+        for r in range(1, SLABS + 1):
+            quantise(r - 1)
+            multiply_slab(r - 1)
+            if r + 1 < SLABS:
+                regroup(r + 1)
+            if r >= FIRST_STATS_STEP and r % 2 == 0:
+                statistics(r - FIRST_STATS_STEP)
+                statistics(r - FIRST_STATS_STEP + 1)
 
         for sample in range((GROUPS - 2) * LANES, (GROUPS - 1) * LANES):
             keep(sample)

@@ -38,6 +38,9 @@ SLAB_1_SCALAR_COLUMNS = 272
 SHARED_SCALAR_COLUMNS = 160
 GPSIMD_COLUMNS = 208
 
+SCALAR_SAMPLE = SAMPLES - 1
+TUPLE = 3
+
 FLOPS = 2 * SAMPLES * OUT_CHANNELS * HEADS * CHANNELS * POSITIONS
 
 
@@ -98,7 +101,10 @@ def tile_block_height_reducing_filtering_pb_t_kernel(
 
         codes = consts.tile([P, SLABS, POSITIONS], U32, align_bytes=64)
         planes = consts.tile([P, SLABS, POSITIONS], U8, align_bytes=64)
-        stats = consts.tile([P, SAMPLES, BN_STATS_DIM], F32)
+        scalar_tuple = BN_STATS_DIM * (SAMPLES - 1)
+        stats = consts.tile([P, scalar_tuple + TUPLE], F32)
+        nc.vector.memset(stats[:, scalar_tuple:], float(POSITIONS))
+        unread = consts.tile([P, POSITIONS], F32)
         grouped = {}
         banks = {}
         kept = {}
@@ -166,7 +172,22 @@ def tile_block_height_reducing_filtering_pb_t_kernel(
                 multiply(sample, n)
 
         def statistics(sample):
-            nc.vector.bn_stats(out=stats[:, sample, :], in_=banks[sample][:])
+            c = BN_STATS_DIM * sample
+            nc.vector.bn_stats(out=stats[:, c : c + BN_STATS_DIM], in_=banks[sample][:])
+
+        def statistics_on_scalar(sample):
+            mean = stats[:, scalar_tuple + 1 : scalar_tuple + 2]
+            nc.scalar.activation(
+                out=unread[:], in_=banks[sample][:], func=ACT.Copy, scale=1.0 / POSITIONS, accum_out=mean
+            )
+            nc.scalar.activation(
+                out=unread[:],
+                in_=banks[sample][:],
+                func=ACT.Square,
+                scale=-1.0,
+                bias=mean,
+                accum_out=stats[:, scalar_tuple + 2 : scalar_tuple + 3],
+            )
 
         def keep(sample):
             kept[sample] = kept_pool.tile([P, POSITIONS], F32, name="kept")
@@ -174,24 +195,38 @@ def tile_block_height_reducing_filtering_pb_t_kernel(
 
         regroup(0)
         regroup(1)
-        for r in range(1, SLABS + 1):
+        for r in range(1, SLABS - 1):
             quantise(r - 1)
             multiply_slab(r - 1)
-            if r + 1 < SLABS:
-                regroup(r + 1)
+            regroup(r + 1)
             if r >= FIRST_STATS_STEP and r % 2 == 0:
                 statistics(r - FIRST_STATS_STEP)
                 statistics(r - FIRST_STATS_STEP + 1)
 
-        for sample in range((GROUPS - 2) * LANES, (GROUPS - 1) * LANES):
-            keep(sample)
+        third, fourth = (GROUPS - 2) * LANES, (GROUPS - 1) * LANES
+        last_group = [SCALAR_SAMPLE] + list(range(fourth, SCALAR_SAMPLE))
+        quantise(SLABS - 2)
+        for sample in last_group[:2]:
+            multiply(sample, HEADS - 2)
+        quantise(SLABS - 1)
+        for sample in last_group[:2]:
+            multiply(sample, HEADS - 1)
+        for sample in last_group[2:]:
+            multiply(sample, HEADS - 2)
+            multiply(sample, HEADS - 1)
+
+        keep(third)
+        keep(third + 1)
+        statistics_on_scalar(SCALAR_SAMPLE)
+        for sample in range(third + 2, SCALAR_SAMPLE):
+            statistics(sample)
+        keep(third + 2)
+        keep(third + 3)
         for sample in range(LANES):
             multiply_again(sample)
-        for sample in range((GROUPS - 1) * LANES, SAMPLES):
-            statistics(sample)
 
         mean_var = consts.tile([P, 2], F32)
-        nc.vector.bn_aggr(out=mean_var[:], in_=stats[:].rearrange("p s c -> p (s c)"))
+        nc.vector.bn_aggr(out=mean_var[:], in_=stats[:])
         std = consts.tile([P, 1], F32)
         nc.scalar.activation(out=std[:], in_=mean_var[:, 1:2], func=ACT.Sqrt, bias=eps[:], scale=1.0)
         minus_g_mean = consts.tile([P, 1], F32)

from contextlib import ExitStack

import concourse.mybir as mybir

BF16 = mybir.dt.bfloat16
F32 = mybir.dt.float32
I32 = mybir.dt.int32
U8 = mybir.dt.uint8
U32 = mybir.dt.uint32
FP8X4 = mybir.dt.float8_e4m3fn_x4
FP4X4 = mybir.dt.float4_e2m1fn_x4
ALU = mybir.AluOpType
ACT = mybir.ActivationFunctionType

HEADS = 4
SAMPLES = 16
CHANNELS = 128
POSITIONS = 512
OUT_CHANNELS = 128
EPS = 1e-5

P = 128
PACK = 4
QUADRANT = CHANNELS // PACK
LANES = P // QUADRANT
SCALE_ROWS = QUADRANT // 8
GROUPS = SAMPLES // LANES
SLABS = GROUPS * HEADS
BANKS = 8
BN_STATS_DIM = 6
EVEN_BUFS = 2
ODD_BUFS = 1

RUN = 4
FIRST_STATS_STEP = LANES + 2
SLAB_0_SCALAR_COLUMNS = 176
SLAB_1_SCALAR_COLUMNS = 272
SHARED_SCALAR_COLUMNS = 160
GPSIMD_COLUMNS = 208

SCALAR_SAMPLE = SAMPLES - 1
TUPLE = 3

FLOPS = 2 * SAMPLES * OUT_CHANNELS * HEADS * CHANNELS * POSITIONS


def tile_block_height_reducing_filtering_pb_t_kernel(
    tc, head_res, W_merge_words, W_merge_scales, g_m, b_m, out
):
    nc = tc.nc
    with ExitStack() as ctx:
        consts = ctx.enter_context(tc.tile_pool(name="consts", bufs=1))
        raw_pool = ctx.enter_context(tc.tile_pool(name="raw", bufs=SLABS))
        even_pool = ctx.enter_context(tc.tile_pool(name="grouped_even", bufs=EVEN_BUFS))
        odd_pool = ctx.enter_context(tc.tile_pool(name="grouped_odd", bufs=ODD_BUFS))
        kept_pool = ctx.enter_context(tc.tile_pool(name="kept", bufs=LANES))
        result_pool = ctx.enter_context(tc.tile_pool(name="result", bufs=SAMPLES))
        psum = ctx.enter_context(tc.psum_pool(name="sums", bufs=BANKS))
        ctx.enter_context(tc.manual_schedule())

        w_scales = consts.tile([P, HEADS, OUT_CHANNELS], U8, align_bytes=64)
        w_words = consts.tile([P, HEADS, LANES, 2 * OUT_CHANNELS], U8, align_bytes=64)
        nc.vector.memset(w_scales[:].rearrange("p n o -> p (n o)").bitcast(I32), 0)
        nc.vector.memset(w_words[:].rearrange("p n j w -> p (n j w)").bitcast(I32), 0)
        eps = consts.tile([P, 1], F32)
        nc.vector.memset(eps[:], EPS)
        warm = consts.tile([P, 1], F32)
        nc.scalar.activation(out=warm[:], in_=eps[:], func=ACT.Sqrt)

        slabs = head_res.rearrange("n (g j) (q t) d -> g n (j q) (t d)", j=LANES, t=PACK)
        raw = {}

        def load(r):
            raw[r] = raw_pool.tile([P, PACK, POSITIONS], BF16, name="raw")
            nc.sync.dma_start(
                out=raw[r][:].rearrange("p t d -> p (t d)"), in_=slabs[r // HEADS, r % HEADS]
            )

        words_by_head = W_merge_words[0].rearrange("(n q) w -> q n w", n=HEADS)
        scales_by_head = W_merge_scales[0].rearrange("(n i) o -> i n o", n=HEADS)
        load(0)
        for j in range(LANES):
            nc.sync.dma_start(
                out=w_scales[QUADRANT * j : QUADRANT * j + SCALE_ROWS, :, :].bitcast(I32),
                in_=scales_by_head.bitcast(I32),
            )
        for r in range(1, LANES):
            load(r)
        for j in range(LANES):
            nc.sync.dma_start(
                out=w_words[QUADRANT * j : QUADRANT * (j + 1), :, j, :].bitcast(I32),
                in_=words_by_head.bitcast(I32),
            )
        for r in range(LANES, SLABS):
            load(r)
        g_bf = consts.tile([P, 1], BF16)
        b_bf = consts.tile([P, 1], BF16)
        with nc.allow_non_contiguous_dma(reason="128 two-byte elements, one to a partition"):
            nc.sync.dma_start(out=g_bf[:], in_=g_m.rearrange("(o one) -> o one", one=1))
            nc.sync.dma_start(out=b_bf[:], in_=b_m.rearrange("(o one) -> o one", one=1))

        codes = consts.tile([P, SLABS, POSITIONS], U32, align_bytes=64)
        planes = consts.tile([P, SLABS, POSITIONS], U8, align_bytes=64)
        scalar_tuple = BN_STATS_DIM * (SAMPLES - 1)
        stats = consts.tile([P, scalar_tuple + TUPLE], F32)
        nc.vector.memset(stats[:, scalar_tuple:], float(POSITIONS))
        unread = consts.tile([P, POSITIONS], F32)
        grouped = {}
        banks = {}
        kept = {}

        def shares(r):
            if r == 0:
                return SLAB_0_SCALAR_COLUMNS, SLAB_0_SCALAR_COLUMNS
            if r == 1:
                return SLAB_1_SCALAR_COLUMNS, SLAB_1_SCALAR_COLUMNS
            if r % 2 == 0:
                return POSITIONS, POSITIONS
            if r <= FIRST_STATS_STEP:
                return 0, 0
            return SHARED_SCALAR_COLUMNS, SHARED_SCALAR_COLUMNS + GPSIMD_COLUMNS

        def regroup(r):
            pool = odd_pool if r % 2 else even_pool
            grouped[r] = pool.tile([P, POSITIONS, PACK], BF16, name="grouped", align_bytes=64)
            src = raw[r][:].rearrange("p t (c i) -> p c t i", i=RUN)
            dst = grouped[r][:].rearrange("p (c i) t -> p c t i", i=RUN)
            first, second = shares(r)
            if first > 0:
                nc.scalar.copy(out=dst[:, : first // RUN], in_=src[:, : first // RUN])
            if second < POSITIONS:
                nc.vector.tensor_copy(out=dst[:, second // RUN :], in_=src[:, second // RUN :])
            if second > first:
                nc.gpsimd.tensor_scalar(
                    out=grouped[r][:, first:second, :],
                    in0=raw[r][:, :, first:second].rearrange("p t d -> p d t"),
                    scalar1=1.0,
                    scalar2=0.0,
                    op0=ALU.mult,
                    op1=ALU.add,
                )

        def quantise(r):
            nc.vector.quantize_mx(
                out=codes[:, r, :].bitcast(FP8X4),
                scales=planes[:, r, :],
                in_=grouped[r][:].rearrange("p d t -> p (d t)"),
            )

        def multiply(sample, n):
            r = (sample // LANES) * HEADS + n
            nc.tensor.matmul_mx(
                out=banks[sample][:],
                lhsT=w_words[:, n, sample % LANES, :].bitcast(FP4X4),
                lhsT_scale=w_scales[:, n, :],
                rhs=codes[:, r, :].bitcast(FP8X4),
                rhs_scale=planes[:, r, :],
                start=(n == 0),
                stop=(n == HEADS - 1),
            )

        def multiply_slab(r):
            g, n = r // HEADS, r % HEADS
            for sample in range(g * LANES, (g + 1) * LANES):
                if n == 0:
                    banks[sample] = psum.tile([P, POSITIONS], F32, name="bank")
                multiply(sample, n)

        def multiply_again(sample):
            banks[sample] = psum.tile([P, POSITIONS], F32, name="bank")
            for n in range(HEADS):
                multiply(sample, n)

        def statistics(sample):
            c = BN_STATS_DIM * sample
            nc.vector.bn_stats(out=stats[:, c : c + BN_STATS_DIM], in_=banks[sample][:])

        def statistics_on_scalar(sample):
            mean = stats[:, scalar_tuple + 1 : scalar_tuple + 2]
            nc.scalar.activation(
                out=unread[:], in_=banks[sample][:], func=ACT.Copy, scale=1.0 / POSITIONS, accum_out=mean
            )
            nc.scalar.activation(
                out=unread[:],
                in_=banks[sample][:],
                func=ACT.Square,
                scale=-1.0,
                bias=mean,
                accum_out=stats[:, scalar_tuple + 2 : scalar_tuple + 3],
            )

        def keep(sample):
            kept[sample] = kept_pool.tile([P, POSITIONS], F32, name="kept")
            nc.scalar.copy(out=kept[sample][:], in_=banks[sample][:])

        regroup(0)
        regroup(1)
        for r in range(1, SLABS - 1):
            quantise(r - 1)
            multiply_slab(r - 1)
            regroup(r + 1)
            if r >= FIRST_STATS_STEP and r % 2 == 0:
                statistics(r - FIRST_STATS_STEP)
                statistics(r - FIRST_STATS_STEP + 1)

        third, fourth = (GROUPS - 2) * LANES, (GROUPS - 1) * LANES
        last_group = [SCALAR_SAMPLE] + list(range(fourth, SCALAR_SAMPLE))
        quantise(SLABS - 2)
        for sample in last_group[:2]:
            multiply(sample, HEADS - 2)
        quantise(SLABS - 1)
        for sample in last_group[:2]:
            multiply(sample, HEADS - 1)
        for sample in last_group[2:]:
            multiply(sample, HEADS - 2)
            multiply(sample, HEADS - 1)

        keep(third)
        keep(third + 1)
        statistics_on_scalar(SCALAR_SAMPLE)
        for sample in range(third + 2, SCALAR_SAMPLE):
            statistics(sample)
        keep(third + 2)
        keep(third + 3)
        for sample in range(LANES):
            multiply_again(sample)

        mean_var = consts.tile([P, 2], F32)
        nc.vector.bn_aggr(out=mean_var[:], in_=stats[:])
        std = consts.tile([P, 1], F32)
        nc.scalar.activation(out=std[:], in_=mean_var[:, 1:2], func=ACT.Sqrt, bias=eps[:], scale=1.0)
        minus_g_mean = consts.tile([P, 1], F32)
        nc.vector.tensor_scalar(
            out=minus_g_mean[:], in0=mean_var[:, 0:1], scalar1=g_bf[:], scalar2=-1.0, op0=ALU.mult, op1=ALU.mult
        )
        rstd = consts.tile([P, 1], F32)
        nc.vector.reciprocal(out=rstd[:], in_=std[:])
        gain = consts.tile([P, 1], F32)
        nc.vector.tensor_mul(out=gain[:], in0=g_bf[:], in1=rstd[:])
        shift = consts.tile([P, 1], F32)
        nc.vector.scalar_tensor_tensor(
            out=shift[:], in0=minus_g_mean[:], scalar=rstd[:], in1=b_bf[:], op0=ALU.mult, op1=ALU.add
        )

        def normalise_bank(sample):
            y = result_pool.tile([P, POSITIONS], F32, name="y")
            nc.scalar.activation(out=y[:], in_=banks[sample][:], func=ACT.Relu, bias=shift[:], scale=gain[:])
            nc.sync.dma_start(out=out[sample], in_=y[:])

        def normalise_kept(sample):
            y = result_pool.tile([P, POSITIONS], F32, name="y")
            nc.vector.tensor_scalar(
                out=y[:], in0=kept[sample][:], scalar1=gain[:], scalar2=shift[:], op0=ALU.mult, op1=ALU.add
            )
            nc.vector.tensor_scalar_max(out=y[:], in0=y[:], scalar1=0.0)
            nc.sync.dma_start(out=out[sample], in_=y[:])

        for j in range(LANES):
            normalise_bank((GROUPS - 1) * LANES + j)
            normalise_kept((GROUPS - 2) * LANES + j)
        for sample in range(LANES):
            normalise_bank(sample)
        for sample in range(LANES, 2 * LANES):
            multiply_again(sample)
            normalise_bank(sample)
